import numpy as np
import ml_dtypes


def mxq(x, axis, fmt="e4m3"):
    dtype, down = {"e4m3": (ml_dtypes.float8_e4m3fn, 7), "e5m2": (ml_dtypes.float8_e5m2, 14)}[fmt]
    v = np.moveaxis(np.asarray(x, np.float32).astype(ml_dtypes.bfloat16).astype(np.float64), axis, -1)
    blocks = v.reshape(v.shape[:-1] + (-1, 32))
    amax = np.abs(blocks).max(-1, keepdims=True)
    byte = np.maximum(np.where(amax > 0, np.frexp(amax)[1] - 1 + 127, 0) - down, 1)
    scale = np.exp2(byte - 127.0)
    codes = (blocks / scale).astype(np.float32).astype(dtype).astype(np.float64)
    return np.moveaxis((codes * scale).reshape(v.shape), -1, axis)


WIDE = False


def mx_kscale(k):
    if not WIDE:
        return np.ones(k)
    levels = np.array([18, -18])
    if k % 512:
        return np.exp2(np.random.permutation(np.resize(levels, k // 32))).repeat(32)
    a = np.empty((k // 512, 16))
    for p in range(k // 512):
        a[p, :8] = np.random.permutation(np.resize(levels, 8))
        for g in range(8):
            far = levels[np.abs(levels - a[p, g]) >= 10]
            a[p, g + 8] = far[np.random.randint(len(far))]
    return np.exp2(a.ravel()).repeat(32)


BF16 = ml_dtypes.bfloat16


def bf(x):
    return np.asarray(x, np.float32).astype(BF16)


def f64(x):
    return np.asarray(x).astype(np.float64)


B, S, H, NH, LAT = 2, 512, 2048, 16, 512
HD = H // NH
HALF = H // 2
R = HALF // 2
T = B * S
ROPE_BASE = 10000.0


def rope_table():
    inv_freq = 1.0 / ROPE_BASE ** (np.arange(0, R, 2) / R)
    freqs = np.outer(np.arange(S), inv_freq)
    emb = np.concatenate([freqs, freqs], -1)
    return np.cos(emb), np.sin(emb)


def apply_rotary(x, cos, sin):
    h = x.shape[-1] // 2
    x1, x2 = x[..., :h], x[..., h:]
    return np.concatenate([x1 * cos - x2 * sin, x1 * sin + x2 * cos], -1)


def apply_rotary_back(g, cos, sin):
    h = g.shape[-1] // 2
    ga, gb = g[..., :h], g[..., h:]
    return np.concatenate([ga * cos + gb * sin, gb * cos - ga * sin], -1)


def setup_inputs():
    s = mx_kscale(T).reshape(B, S, 1)
    u = np.tile(mx_kscale(HALF)[:R], 2)
    v = mx_kscale(LAT)
    cos, sin = rope_table()
    x0 = bf(np.random.standard_normal((B, S, H)))
    wd0 = bf(np.random.standard_normal((LAT, H)) / np.sqrt(H))
    bd = bf(np.random.standard_normal(LAT) * 0.2)
    wu0 = bf(np.random.standard_normal((HALF, LAT)) * 1.2 / np.sqrt(LAT))
    bu = bf(np.random.standard_normal(HALF) * 0.2)
    g = np.random.standard_normal((B, S, H)) * np.exp2(np.random.randint(-6, 1, (B, S, 1)))
    g = g / s * np.concatenate([u, u])
    g = np.ascontiguousarray(g.reshape(B, S, NH, HD).transpose(0, 2, 1, 3))
    q_lat = f64(x0) @ f64(wd0).T + f64(bd)
    return {"hidden_states": bf(f64(x0) * s),
            "Wq_down": bf(f64(wd0) / v[:, None]),
            "bq_down": bd,
            "Wq_up": bf(f64(wu0) * v / u[:, None]),
            "bq_up": bu,
            "rope_cos": bf(cos),
            "rope_sin": bf(sin),
            "q_lat": np.asarray(q_lat, np.float32),
            "grad_out": bf(g)}


def reference(hidden_states, Wq_down, bq_down, Wq_up, bq_up, rope_cos, rope_sin, q_lat, grad_out):
    x = f64(hidden_states).reshape(T, H)
    g = f64(grad_out).transpose(0, 2, 1, 3).reshape(B, S, H)
    dz2 = g[..., :HALF] + apply_rotary_back(g[..., HALF:], f64(rope_cos), f64(rope_sin))
    dz2 = dz2.reshape(T, HALF)
    dz1 = mxq(dz2, 1, "e5m2") @ mxq(f64(Wq_up), 0, "e4m3")
    dx = mxq(dz1, 1, "e5m2") @ mxq(f64(Wq_down), 0, "e4m3")
    dw = mxq(dz1, 0, "e5m2").T @ mxq(x, 0, "e4m3")
    return dx.reshape(B, S, H), dw

@@ -1,0 +1,526 @@
+from contextlib import ExitStack
+
+import concourse.mybir as mybir
+from concourse.masks import make_identity
+
+F32 = mybir.dt.float32
+BF16 = mybir.dt.bfloat16
+U32 = mybir.dt.uint32
+U8 = mybir.dt.uint8
+E4 = mybir.dt.float8_e4m3fn_x4
+E5 = mybir.dt.float8_e5m2_x4
+MULT = mybir.AluOpType.mult
+
+P = 128
+B, S, H, LAT, HALF = 2, 512, 2048, 512, 1024
+J = 4
+N = 512
+
+FLOPS = 2 * B * S * HALF * LAT + 4 * B * S * LAT * H
+BYTES = 2 * (B * S * H * 2 + LAT * H + HALF * LAT + 2 * S * 512) + 4 * (B * S * H + LAT * H)
+
+
+def tile_multiheadlatentattention_pa_v_kernel(
+    tc, hidden_states, Wq_down, bq_down, Wq_up, bq_up, rope_cos, rope_sin, q_lat, grad_out, out_0, out_1
+):
+    nc = tc.nc
+    with ExitStack() as ctx:
+        keep = ctx.enter_context(tc.tile_pool(name="keep", bufs=1))
+        raws = ctx.enter_context(tc.tile_pool(name="raws", bufs=7))
+        prods = ctx.enter_context(tc.tile_pool(name="prods", bufs=14))
+        work = ctx.enter_context(tc.tile_pool(name="work", bufs=2))
+        outs = ctx.enter_context(tc.tile_pool(name="outs", bufs=4))
+        psum = ctx.enter_context(tc.psum_pool(name="psum", bufs=2))
+
+        ident = keep.tile([P, P], F32, name="ident")
+        make_identity(nc, ident[:])
+        ctx.enter_context(tc.manual_schedule())
+
+        def raw(name):
+            return raws.tile([P, 4096], BF16, name=name, tag="raw", align_bytes=64)
+
+        def load_table(src, k):
+            nc.sync.dma_start(out=cs[:, k * 2048 : k * 2048 + 2048], in_=src.rearrange("(p j) c -> p (j c)", j=J))
+
+        def load_g(b, h0, dst, k):
+            src = grad_out[b].rearrange("h (p j) d -> p h (j d)", j=J)
+            nc.sync.dma_start(
+                out=dst[:, k * 2048 : k * 2048 + 2048].rearrange("p (h f) -> p h f", h=4), in_=src[:, h0 : h0 + 4, :]
+            )
+
+        def load_wu(g):
+            nc.sync.dma_start(
+                out=wu_raw[:, g * 2048 : g * 2048 + 2048],
+                in_=Wq_up.rearrange("(g p j) l -> g p (j l)", g=2, j=J)[g],
+            )
+
+        def load_rows(src, w0, name):
+            t = raw(name)
+            nc.sync.dma_start(
+                out=t[:].rearrange("p (j w) -> p j w", j=J),
+                in_=src.rearrange("(p j) w -> p j w", j=J)[:, :, w0 : w0 + 1024],
+            )
+            return t
+
+        cs = keep.tile([P, 4096], BF16, name="cs", align_bytes=64)
+        r0 = raw("r0")
+        wu_raw = raw("wu_raw")
+        load_wu(0)
+        load_table(rope_cos, 0)
+        load_g(0, 8, r0, 0)
+        load_g(0, 12, r0, 1)
+        load_table(rope_sin, 1)
+        d0 = raw("d0")
+        load_g(0, 0, d0, 0)
+        load_g(0, 4, d0, 1)
+        load_wu(1)
+        wd_raw = [load_rows(Wq_down, 0, "wd_raw0"), load_rows(Wq_down, 1024, "wd_raw1")]
+        r1 = raw("r1")
+        load_g(1, 8, r1, 0)
+        load_g(1, 12, r1, 1)
+        d1 = raw("d1")
+        load_g(1, 0, d1, 0)
+        load_g(1, 4, d1, 1)
+        x_raw = {}
+        for half in range(2):
+            for b in range(B):
+                x_raw[b, half] = load_rows(hidden_states[b], half * 1024, "x_raw%d%d" % (b, half))
+
+        nsin = keep.tile([P, 2048], BF16, name="nsin")
+        cosv = cs[:, 0:2048].rearrange("p (j h d t) -> p j t h d", j=J, h=4, t=4)
+        sinv = cs[:, 2048:4096].rearrange("p (j h d t) -> p j t h d", j=J, h=4, t=4)
+        nsinv = nsin[:].rearrange("p (j h d t) -> p j t h d", j=J, h=4, t=4)
+        grot = [t[:].rearrange("p (k h j d t) -> p k j t h d", k=2, h=4, j=J, t=4) for t in (r0, r1)]
+        gdir = [t[:].rearrange("p (k h j d t) -> p k j t h d", k=2, h=4, j=J, t=4) for t in (d0, d1)]
+
+        def interleave(eng, dst, src):
+            d = dst.rearrange("p (c i t) -> p c t i", i=4, t=4)
+            s = src.rearrange("p t (c i) -> p c t i", i=4)
+            if eng == "s":
+                nc.scalar.copy(out=d, in_=s)
+            else:
+                nc.vector.tensor_copy(out=d, in_=s)
+
+        def q_tiles(name, width):
+            codes = keep.tile([P, width], U32, name=name + "q", align_bytes=64)
+            scales = keep.tile([P, width], U8, name=name + "s", align_bytes=64)
+            return codes, scales
+
+        wu = [q_tiles("wu%d" % g, LAT) for g in range(2)]
+        wd = q_tiles("wd", H)
+        xx = [q_tiles("x%d" % b, H) for b in range(B)]
+        lat = [q_tiles("lat%d" % b, N) for b in range(B)]
+        tok = [q_tiles("tok%d" % b, N) for b in range(B)]
+        z = {}
+        zz = {}
+        pr = {}
+        srt = {}
+        bank = {}
+        il = {}
+        dd = {}
+        tt = {}
+        st = {}
+
+        def negate():
+            nc.vector.tensor_scalar(out=nsin[:], in0=cs[:, 2048:4096], scalar1=-1.0, scalar2=None, op0=MULT)
+
+        def mult(b, j, g, k):
+            c = (cosv, sinv)[k] if g == 0 else (nsinv, cosv)[k]
+            t = prods.tile([P, 4, 4, 32], F32, name="pr", tag="pr", bufs=14)
+            nc.vector.tensor_tensor(out=t[:], in0=grot[b][:, k, j], in1=c[:, j], op=MULT)
+            pr[b, j, g, k] = t
+
+        def sort(b, g, half, eng):
+            if half == 0:
+                srt[b, g] = prods.tile([P, J, 4, 4, 32], F32, name="ps", tag="ps", bufs=2)
+            js = slice(2 * half, 2 * half + 2)
+            drain(eng, srt[b, g][:, js], gdir[b][:, g, js])
+
+        def turn(b, j, g):
+            t = psum.tile([P, 4, P], F32, name="tp", tag="tp", bufs=3)
+            for i in range(4):
+                terms = (pr[b, j, g, 0][:, i], pr[b, j, g, 1][:, i], srt[b, g][:, j, i])
+                for n, term in enumerate(terms):
+                    nc.tensor.matmul(
+                        out=t[:, i, :],
+                        lhsT=term.rearrange("p h d -> p (h d)"),
+                        rhs=ident[:],
+                        is_transpose=True,
+                        start=(n == 0),
+                        stop=(n == 2),
+                    )
+            bank[b, j, g] = t
+
+        def turn_out(b, j, g):
+            if j == 0:
+                z[b, g] = work.tile([P, 2048], BF16, name="z", tag="z", bufs=2, align_bytes=64)
+            nc.scalar.copy(
+                out=z[b, g][:, j * 512 : j * 512 + 512].rearrange("p (r t) -> p r t", t=4),
+                in_=bank[b, j, g][:].rearrange("p t r -> p r t"),
+            )
+
+        def quant_z(b, g, half):
+            if half == 0:
+                zq = work.tile([P, N], U32, name="zq", tag="zq", bufs=4, align_bytes=64)
+                zs = work.tile([P, N], U8, name="zs", tag="zs", bufs=4, align_bytes=64)
+                zz[b, g] = (zq, zs)
+            c = slice(half * 256, half * 256 + 256)
+            nc.vector.quantize_mx(
+                out=zz[b, g][0][:, c].bitcast(E5),
+                scales=zz[b, g][1][:, c],
+                in_=z[b, g][:, half * 1024 : half * 1024 + 1024],
+            )
+
+        def mx(out, lhs, m, rhs, c, start, stop):
+            nc.tensor.matmul_mx(
+                out=out,
+                lhsT=lhs[0][:, m * P : m * P + P].bitcast(E5),
+                lhsT_scale=lhs[1][:, m * P : m * P + P],
+                rhs=rhs[0][:, c].bitcast(E4),
+                rhs_scale=rhs[1][:, c],
+                start=start,
+                stop=stop,
+            )
+
+        def dh(b, j):
+            t = psum.tile([P, LAT], F32, name="dh", tag="dh", bufs=2)
+            for g in range(2):
+                mx(t[:], zz[b, g], j, wu[g], slice(0, LAT), g == 0, g == 1)
+            bank["dh", b, j] = t
+
+        def dh_out(b, j):
+            if j == 0:
+                dd[b] = work.tile([P, J, LAT], BF16, name="d", tag="d", bufs=2, align_bytes=64)
+            nc.scalar.copy(out=dd[b][:, j, :], in_=bank["dh", b, j][:])
+
+        def turn_words(b, half):
+            words = dd[b][:].rearrange("p j l -> p (j l)").bitcast(F32)
+            t = psum.tile([P, 2, 2, P], F32, name="tb", tag="tp", bufs=3)
+            for k in range(2):
+                for u in range(2):
+                    w0 = (2 * half + k) * 256 + u
+                    nc.tensor.transpose(t[:, k, u, :], words[:, w0 : w0 + 255 : 2], ident[:])
+            bank["w", b, half] = t
+
+        def words_out(b, half):
+            if half == 0:
+                tt[b] = work.tile([P, 2048], BF16, name="tt", tag="tt", bufs=2, align_bytes=64)
+            nc.scalar.copy(
+                out=tt[b][:, half * 1024 : half * 1024 + 1024].bitcast(F32).rearrange("p (k r u) -> p k r u", k=2, u=2),
+                in_=bank["w", b, half][:].rearrange("p k u r -> p k r u"),
+            )
+
+        def quant(dst, c, src, dt):
+            nc.vector.quantize_mx(out=dst[0][:, c].bitcast(dt), scales=dst[1][:, c], in_=src)
+
+        def quant_lat(b):
+            quant(lat[b], slice(0, N), tt[b][:], E5)
+
+        def il_tile(key, eng):
+            il[key] = work.tile([P, 2048], BF16, name="il", tag="il" + eng, bufs=2, align_bytes=64)
+            return il[key][:]
+
+        def il_tok(b):
+            interleave("v", il_tile(("tok", b), "v"), dd[b][:])
+
+        def quant_tok(b):
+            quant(tok[b], slice(0, N), il["tok", b][:], E5)
+
+        def il_wu(g, eng):
+            interleave(eng, il_tile(("wu", g), eng), wu_raw[:, g * 2048 : g * 2048 + 2048].rearrange("p (t w) -> p t w", t=4))
+
+        def quant_wu(g):
+            quant(wu[g], slice(0, LAT), il["wu", g][:], E4)
+
+        def il_rows(eng, key, src, n):
+            v = src[:].rearrange("p (t w) -> p t w", t=4)
+            interleave(eng, il_tile((key, n), eng), v[:, :, (n % 2) * 512 : (n % 2) * 512 + 512])
+
+        def il_wd(n, eng):
+            il_rows(eng, "wd", wd_raw[n // 2], n)
+
+        def quant_wd(n):
+            quant(wd, slice(n * N, n * N + N), il["wd", n][:], E4)
+
+        def il_x(b, n, eng):
+            il_rows(eng, b, x_raw[b, n // 2], n)
+
+        def quant_x(b, n):
+            quant(xx[b], slice(n * N, n * N + N), il[b, n][:], E4)
+
+        def drain(eng, dst, src):
+            if eng == "s":
+                nc.scalar.copy(out=dst, in_=src)
+            else:
+                nc.vector.tensor_copy(out=dst, in_=src)
+
+        def out0(b, j, n):
+            t = psum.tile([P, N], F32, name="ob", tag="ob", bufs=3)
+            mx(t[:], lat[b], j, wd, slice(n * N, n * N + N), True, True)
+            bank["o0", b, j, n] = t
+
+        def out0_out(b, j, n, eng):
+            if n % 2 == 0:
+                st[b, j] = outs.tile([P, 1024], F32, name="st", tag="st", bufs=4)
+            drain(eng, st[b, j][:, (n % 2) * N : (n % 2) * N + N], bank["o0", b, j, n][:])
+
+        def out0_store(b, j, n):
+            nc.sync.dma_start(
+                out=out_0[b].rearrange("(p j) w -> p j w", j=J)[:, j, (n - 1) * N : (n + 1) * N], in_=st[b, j][:]
+            )
+
+        def out1(m, n):
+            t = psum.tile([P, N], F32, name="ob", tag="ob", bufs=3)
+            for b in range(B):
+                mx(t[:], tok[b], m, xx[b], slice(n * N, n * N + N), b == 0, b == 1)
+            bank["o1", m, n] = t
+
+        def out1_out(m, n, eng):
+            st["o1", m, n] = outs.tile([P, N], F32, name="s1", tag="s1", bufs=6)
+            drain(eng, st["o1", m, n][:], bank["o1", m, n][:])
+
+        def out1_store(m, n):
+            nc.sync.dma_start(out=out_1[m * P : m * P + P, n * N : n * N + N], in_=st["o1", m, n][:])
+
+        vec, sca, ten, dma = [], [], [], []
+
+        def put(stream, key, needs, fn, *args):
+            stream.append((key, needs, fn, args))
+
+        def v_mult(b, j, g, k):
+            needs = [("neg",)] if (g == 1 and k == 0) else []
+            put(vec, ("mult", b, j, g, k), needs, mult, b, j, g, k)
+
+        def v_sort(b, g, h):
+            put(vec, ("sort", b, g, h), [], sort, b, g, h, "v")
+
+        def s_sort(b, g, h):
+            put(sca, ("sort", b, g, h), [], sort, b, g, h, "s")
+
+        def v_quant_z(b, h):
+            for g in range(2):
+                put(vec, ("qz", b, g, h), [("zo", b, 2 * h + 1, g)], quant_z, b, g, h)
+
+        def v_wu(g):
+            put(vec, ("qwu", g), [("ilwu", g)], quant_wu, g)
+
+        def v_wd(n):
+            put(vec, ("qwd", n), [("ilwd", n)], quant_wd, n)
+
+        def v_x(b, n):
+            put(vec, ("ilx", b, n), [], il_x, b, n, "v")
+
+        def v_qx(b, n):
+            put(vec, ("qx", b, n), [("ilx", b, n)], quant_x, b, n)
+
+        def v_qlat(b):
+            put(vec, ("qlat", b), [("wo", b, 1)], quant_lat, b)
+
+        def v_iltok(b):
+            put(vec, ("iltok", b), [("dho", b, 3)], il_tok, b)
+
+        def v_qtok(b):
+            put(vec, ("qtok", b), [("iltok", b)], quant_tok, b)
+
+        def v_o1(m, n):
+            put(vec, ("o1o", m, n), [("o1", m, n)], out1_out, m, n, "v")
+
+        def v_o0(b, j, n):
+            put(vec, ("o0o", b, j, n), [("o0", b, j, n)], out0_out, b, j, n, "v")
+
+        def v_ilwu(g):
+            put(vec, ("ilwu", g), [], il_wu, g, "v")
+
+        def v_ilwd(n):
+            put(vec, ("ilwd", n), [], il_wd, n, "v")
+
+        def s_wu(g):
+            put(sca, ("ilwu", g), [], il_wu, g, "s")
+
+        def s_wd(n):
+            put(sca, ("ilwd", n), [], il_wd, n, "s")
+
+        def s_x(b, n):
+            put(sca, ("ilx", b, n), [], il_x, b, n, "s")
+
+        def s_z(b, j, g):
+            put(sca, ("zo", b, j, g), [("turn", b, j, g)], turn_out, b, j, g)
+
+        def s_dh(b, j):
+            put(sca, ("dho", b, j), [("dh", b, j)], dh_out, b, j)
+
+        def s_words(b, h):
+            put(sca, ("wo", b, h), [("words", b, h)], words_out, b, h)
+
+        def s_o0(b, j, n):
+            put(sca, ("o0o", b, j, n), [("o0", b, j, n)], out0_out, b, j, n, "s")
+
+        def s_o1(m, n):
+            put(sca, ("o1o", m, n), [("o1", m, n)], out1_out, m, n, "s")
+
+        def t_turn(b, j, g):
+            needs = [("mult", b, j, g, 0), ("mult", b, j, g, 1), ("sort", b, g, j // 2)]
+            put(ten, ("turn", b, j, g), needs, turn, b, j, g)
+
+        def t_dh(b, j):
+            put(ten, ("dh", b, j), [("qz", b, g, j // 2) for g in range(2)] + [("qwu", 0), ("qwu", 1)], dh, b, j)
+
+        def t_words(b, h):
+            put(ten, ("words", b, h), [("dho", b, 2 * h + 1)], turn_words, b, h)
+
+        def t_o0(b, j, n):
+            put(ten, ("o0", b, j, n), [("qlat", b), ("qwd", n)], out0, b, j, n)
+            if n % 2 == 1:
+                put(dma, ("o0s", b, j, n), [("o0o", b, j, n)], out0_store, b, j, n)
+
+        def t_o1(m, n):
+            put(ten, ("o1", m, n), [("qtok", 0), ("qtok", 1), ("qx", 0, n), ("qx", 1, n)], out1, m, n)
+            put(dma, ("o1s", m, n), [("o1o", m, n)], out1_store, m, n)
+
+        def o0(eng, b, j, n):
+            t_o0(b, j, n)
+            (s_o0 if eng == "s" else v_o0)(b, j, n)
+
+        def o1(eng, m, n):
+            t_o1(m, n)
+            (s_o1 if eng == "s" else v_o1)(m, n)
+
+        def zt(b, j, g):
+            t_turn(b, j, g)
+            s_z(b, j, g)
+
+        def dhs(b, h):
+            for j in (2 * h, 2 * h + 1):
+                t_dh(b, j)
+                s_dh(b, j)
+
+        def ws(b, h):
+            t_words(b, h)
+            s_words(b, h)
+
+        v_ilwu(0)
+        for j in range(J):
+            v_mult(0, j, 0, 0)
+            if j == 0:
+                v_wu(0)
+        for j in range(J):
+            v_mult(0, j, 1, 1)
+        put(vec, ("neg",), [], negate)
+        for j in range(J):
+            v_mult(0, j, 0, 1)
+            v_mult(0, j, 1, 0)
+            if j == 1:
+                v_ilwu(1)
+            if j == 2:
+                v_wu(1)
+        v_ilwd(0)
+        v_quant_z(0, 0)
+        v_ilwd(1)
+        v_wd(0)
+        v_quant_z(0, 1)
+        v_ilwd(2)
+        v_wd(1)
+        s_sort(0, 0, 0)
+        s_sort(0, 1, 0)
+        zt(0, 0, 0)
+        s_sort(0, 0, 1)
+        zt(0, 0, 1)
+        zt(0, 1, 0)
+        zt(0, 1, 1)
+        s_sort(0, 1, 1)
+        zt(0, 2, 0)
+        zt(0, 2, 1)
+        dhs(0, 0)
+        zt(0, 3, 0)
+        ws(0, 0)
+        zt(0, 3, 1)
+        s_wd(3)
+        dhs(0, 1)
+        s_sort(1, 0, 0)
+        ws(0, 1)
+        s_sort(1, 1, 0)
+        for j in range(J):
+            v_mult(1, j, 0, 0)
+            v_mult(1, j, 0, 1)
+            if j == 0:
+                v_wd(2)
+                v_qlat(0)
+                v_wd(3)
+            if j == 2:
+                v_sort(1, 0, 1)
+            v_mult(1, j, 1, 0)
+            v_mult(1, j, 1, 1)
+            if j == 2:
+                v_sort(1, 1, 1)
+                v_iltok(0)
+            if j == 3:
+                v_quant_z(1, 0)
+                v_qtok(0)
+        for n in range(4):
+            o0("s", 0, 0, n)
+        zt(1, 0, 0)
+        zt(1, 0, 1)
+        for j in range(1, 3):
+            for n in range(4):
+                if n % 2 == 0:
+                    zt(1, j, n // 2)
+                o0("s", 0, j, n)
+        zt(1, 3, 0)
+        o0("s", 0, 3, 0)
+        o0("s", 0, 3, 1)
+        zt(1, 3, 1)
+        v_x(0, 0)
+        v_quant_z(1, 1)
+        v_x(1, 0)
+        v_qx(0, 0)
+        dhs(1, 0)
+        ws(1, 0)
+        dhs(1, 1)
+        ws(1, 1)
+        o0("s", 0, 3, 2)
+        o0("s", 0, 3, 3)
+        v_qlat(1)
+        v_qx(1, 0)
+        v_iltok(1)
+        v_x(0, 1)
+        v_qtok(1)
+        for n in range(4):
+            o0("s", 1, 0, n)
+        v_x(1, 1)
+        v_qx(0, 1)
+        for n in range(4):
+            o0("s", 1, 1, n)
+        v_qx(1, 1)
+        v_x(0, 2)
+        for m in range(4):
+            o1("s", m, 0)
+        v_x(1, 2)
+        v_qx(0, 2)
+        for n in range(4):
+            o0("s", 1, 2, n)
+        v_qx(1, 2)
+        v_x(0, 3)
+        for m in range(4):
+            o1("s", m, 1)
+        v_x(1, 3)
+        v_qx(0, 3)
+        for n in range(4):
+            o0("s", 1, 3, n)
+        v_qx(1, 3)
+        for n in range(2, 4):
+            for m in range(4):
+                o1("v" if m % 2 else "s", m, n)
+
+        done = {}
+        streams = [vec, sca, ten, dma]
+        at = [0, 0, 0, 0]
+        while any([at[i] < len(streams[i]) for i in range(4)]):
+            before = list(at)
+            for i in range(4):
+                if at[i] < len(streams[i]):
+                    key, needs, fn, args = streams[i][at[i]]
+                    if all([k in done for k in needs]):
+                        fn(*args)
+                        done[key] = True
+                        at[i] += 1
+            assert at != before, [streams[i][at[i]][:2] for i in range(4) if at[i] < len(streams[i])]

@@ -34,6 +34,8 @@ def tile_multiheadlatentattention_pa_v_kernel(
 
         ident = keep.tile([P, P], F32, name="ident")
         make_identity(nc, ident[:])
+        ident_b = keep.tile([P, P], BF16, name="ident_b")
+        make_identity(nc, ident_b[:])
         ctx.enter_context(tc.manual_schedule())
 
         def raw(name):
@@ -68,12 +70,12 @@ def tile_multiheadlatentattention_pa_v_kernel(
         load_wu(0)
         load_table(rope_cos, 0)
         load_g(0, 8, r0, 0)
+        load_wu(1)
         load_g(0, 12, r0, 1)
         load_table(rope_sin, 1)
         d0 = raw("d0")
         load_g(0, 0, d0, 0)
         load_g(0, 4, d0, 1)
-        load_wu(1)
         wd_raw = [load_rows(Wq_down, 0, "wd_raw0"), load_rows(Wq_down, 1024, "wd_raw1")]
         r1 = raw("r1")
         load_g(1, 8, r1, 0)
@@ -132,24 +134,38 @@ def tile_multiheadlatentattention_pa_v_kernel(
 
         def sort(b, g, half, eng):
             if half == 0:
-                srt[b, g] = prods.tile([P, J, 4, 4, 32], F32, name="ps", tag="ps", bufs=2)
+                srt[b, g] = prods.tile([P, J, 4, 4, 32], BF16, name="ps", tag="ps", bufs=2)
             js = slice(2 * half, 2 * half + 2)
             drain(eng, srt[b, g][:, js], gdir[b][:, g, js])
 
         def turn(b, j, g):
             t = psum.tile([P, 4, P], F32, name="tp", tag="tp", bufs=3)
             for i in range(4):
-                terms = (pr[b, j, g, 0][:, i], pr[b, j, g, 1][:, i], srt[b, g][:, j, i])
-                for n, term in enumerate(terms):
+                nc.tensor.matmul(
+                    out=t[:, i, :],
+                    lhsT=srt[b, g][:, j, i].rearrange("p h d -> p (h d)"),
+                    rhs=ident_b[:],
+                    start=(i == 0),
+                    stop=False,
+                )
+            for k in range(2):
+                for i in range(4):
                     nc.tensor.matmul(
                         out=t[:, i, :],
-                        lhsT=term.rearrange("p h d -> p (h d)"),
+                        lhsT=pr[b, j, g, k][:, i].rearrange("p h d -> p (h d)"),
                         rhs=ident[:],
                         is_transpose=True,
-                        start=(n == 0),
-                        stop=(n == 2),
+                        start=False,
+                        stop=(k == 1 and i == 3),
                     )
             bank[b, j, g] = t
+
+        def warm(src, c0):
+            if "warm" not in bank:
+                bank["warm"] = psum.tile([P, N], F32, name="warm", tag="dh", bufs=2)
+            nc.tensor.matmul(
+                out=bank["warm"][:], lhsT=src[:, c0 : c0 + P], rhs=src[:, c0 : c0 + N], start=True, stop=True
+            )
 
         def turn_out(b, j, g):
             if j == 0:
@@ -217,7 +233,7 @@ def tile_multiheadlatentattention_pa_v_kernel(
             quant(lat[b], slice(0, N), tt[b][:], E5)
 
         def il_tile(key, eng):
-            il[key] = work.tile([P, 2048], BF16, name="il", tag="il" + eng, bufs=2, align_bytes=64)
+            il[key] = work.tile([P, 2048], BF16, name="il", tag="il" + eng, bufs=3, align_bytes=64)
             return il[key][:]
 
         def il_tok(b):
@@ -398,11 +414,12 @@ def tile_multiheadlatentattention_pa_v_kernel(
             t_words(b, h)
             s_words(b, h)
 
-        v_ilwu(0)
+        for n, (src, c0) in enumerate(((r0, 0), (r0, 2048), (cs, 2048), (d0, 0), (d0, 2048))):
+            for i in range(2):
+                put(ten, ("warm", n, i), [], warm, src, c0)
         for j in range(J):
             v_mult(0, j, 0, 0)
-            if j == 0:
-                v_wu(0)
+        v_wu(0)
         for j in range(J):
             v_mult(0, j, 1, 1)
         put(vec, ("neg",), [], negate)
@@ -410,83 +427,92 @@ def tile_multiheadlatentattention_pa_v_kernel(
             v_mult(0, j, 0, 1)
             v_mult(0, j, 1, 0)
             if j == 1:
-                v_ilwu(1)
-            if j == 2:
                 v_wu(1)
+                v_sort(0, 0, 1)
+                v_sort(0, 1, 1)
         v_ilwd(0)
+        v_mult(1, 0, 0, 0)
         v_quant_z(0, 0)
-        v_ilwd(1)
         v_wd(0)
-        v_quant_z(0, 1)
-        v_ilwd(2)
+        v_mult(1, 0, 0, 1)
+        v_ilwd(1)
+        v_mult(1, 0, 1, 0)
         v_wd(1)
+        v_quant_z(0, 1)
+        v_mult(1, 0, 1, 1)
+        v_mult(1, 1, 0, 0)
+        v_mult(1, 1, 0, 1)
+        s_wu(0)
+        s_wu(1)
         s_sort(0, 0, 0)
         s_sort(0, 1, 0)
         zt(0, 0, 0)
-        s_sort(0, 0, 1)
         zt(0, 0, 1)
         zt(0, 1, 0)
         zt(0, 1, 1)
-        s_sort(0, 1, 1)
+        s_wd(2)
         zt(0, 2, 0)
         zt(0, 2, 1)
         dhs(0, 0)
         zt(0, 3, 0)
         ws(0, 0)
         zt(0, 3, 1)
-        s_wd(3)
-        dhs(0, 1)
         s_sort(1, 0, 0)
-        ws(0, 1)
+        dhs(0, 1)
         s_sort(1, 1, 0)
-        for j in range(J):
-            v_mult(1, j, 0, 0)
-            v_mult(1, j, 0, 1)
-            if j == 0:
-                v_wd(2)
-                v_qlat(0)
-                v_wd(3)
+        ws(0, 1)
+        for j in range(1, J):
+            if j > 1:
+                v_mult(1, j, 0, 0)
+                v_mult(1, j, 0, 1)
             if j == 2:
                 v_sort(1, 0, 1)
+                v_ilwd(3)
             v_mult(1, j, 1, 0)
             v_mult(1, j, 1, 1)
+            if j == 1:
+                v_wd(2)
+                v_qlat(0)
             if j == 2:
+                v_wd(3)
                 v_sort(1, 1, 1)
                 v_iltok(0)
             if j == 3:
                 v_quant_z(1, 0)
                 v_qtok(0)
-        for n in range(4):
-            o0("s", 0, 0, n)
         zt(1, 0, 0)
+        o0("s", 0, 0, 0)
+        o0("s", 0, 0, 1)
         zt(1, 0, 1)
         for j in range(1, 3):
-            for n in range(4):
-                if n % 2 == 0:
-                    zt(1, j, n // 2)
-                o0("s", 0, j, n)
+            for g in range(2):
+                zt(1, j, g)
+                o0("s", 0, j, 2 * g)
+                o0("s", 0, j, 2 * g + 1)
+        o0("s", 0, 0, 2)
+        o0("s", 0, 0, 3)
         zt(1, 3, 0)
         o0("s", 0, 3, 0)
         o0("s", 0, 3, 1)
         zt(1, 3, 1)
         v_x(0, 0)
-        v_quant_z(1, 1)
         v_x(1, 0)
+        v_quant_z(1, 1)
         v_qx(0, 0)
         dhs(1, 0)
+        o0("s", 0, 3, 2)
         ws(1, 0)
         dhs(1, 1)
-        ws(1, 1)
-        o0("s", 0, 3, 2)
         o0("s", 0, 3, 3)
-        v_qlat(1)
+        ws(1, 1)
         v_qx(1, 0)
-        v_iltok(1)
         v_x(0, 1)
+        v_iltok(1)
+        v_qlat(1)
+        v_x(1, 1)
         v_qtok(1)
         for n in range(4):
             o0("s", 1, 0, n)
-        v_x(1, 1)
         v_qx(0, 1)
         for n in range(4):
             o0("s", 1, 1, n)
@@ -504,12 +530,14 @@ def tile_multiheadlatentattention_pa_v_kernel(
             o1("s", m, 1)
         v_x(1, 3)
         v_qx(0, 3)
-        for n in range(4):
-            o0("s", 1, 3, n)
         v_qx(1, 3)
-        for n in range(2, 4):
-            for m in range(4):
-                o1("v" if m % 2 else "s", m, n)
+        for n in range(2):
+            o1("s", 2 * n, 2)
+            o0("v", 1, 3, 2 * n)
+            o1("s", 2 * n + 1, 2)
+            o0("v", 1, 3, 2 * n + 1)
+        for m in range(4):
+            o1("v" if m % 2 else "s", m, 3)
 
         done = {}
         streams = [vec, sca, ten, dma]

@@ -276,13 +276,13 @@ def tile_multiheadlatentattention_pa_v_kernel(
             bank["o0", b, j, n] = t
 
         def out0_out(b, j, n, eng):
-            if n % 2 == 0:
-                st[b, j] = outs.tile([P, 1024], F32, name="st", tag="st", bufs=4)
-            drain(eng, st[b, j][:, (n % 2) * N : (n % 2) * N + N], bank["o0", b, j, n][:])
+            if (b, j, n // 2) not in st:
+                st[b, j, n // 2] = outs.tile([P, 1024], F32, name="st", tag="st", bufs=4)
+            drain(eng, st[b, j, n // 2][:, (n % 2) * N : (n % 2) * N + N], bank["o0", b, j, n][:])
 
         def out0_store(b, j, n):
             nc.sync.dma_start(
-                out=out_0[b].rearrange("(p j) w -> p j w", j=J)[:, j, (n - 1) * N : (n + 1) * N], in_=st[b, j][:]
+                out=out_0[b].rearrange("(p j) w -> p j w", j=J)[:, j, (n - 1) * N : (n + 1) * N], in_=st[b, j, n // 2][:]
             )
 
         def out1(m, n):
@@ -376,6 +376,8 @@ def tile_multiheadlatentattention_pa_v_kernel(
 
         def t_turn(b, j, g):
             needs = [("mult", b, j, g, 0), ("mult", b, j, g, 1), ("sort", b, g, j // 2)]
+            if b == 0:
+                put(ten, ("warm", j, g, "t"), needs, warm, r0, 0)
             put(ten, ("turn", b, j, g), needs, turn, b, j, g)
 
         def t_dh(b, j):
@@ -387,7 +389,7 @@ def tile_multiheadlatentattention_pa_v_kernel(
         def t_o0(b, j, n):
             put(ten, ("o0", b, j, n), [("qlat", b), ("qwd", n)], out0, b, j, n)
             if n % 2 == 1:
-                put(dma, ("o0s", b, j, n), [("o0o", b, j, n)], out0_store, b, j, n)
+                put(dma, ("o0s", b, j, n), [("o0o", b, j, n - 1), ("o0o", b, j, n)], out0_store, b, j, n)
 
         def t_o1(m, n):
             put(ten, ("o1", m, n), [("qtok", 0), ("qtok", 1), ("qx", 0, n), ("qx", 1, n)], out1, m, n)
@@ -414,8 +416,8 @@ def tile_multiheadlatentattention_pa_v_kernel(
             t_words(b, h)
             s_words(b, h)
 
-        for n, (src, c0) in enumerate(((r0, 0), (r0, 2048), (cs, 2048), (d0, 0), (d0, 2048))):
-            for i in range(2):
+        for n, (src, c0, times) in enumerate(((r0, 2048, 2), (cs, 2048, 1), (d0, 0, 2), (d0, 2048, 2))):
+            for i in range(times):
                 put(ten, ("warm", n, i), [], warm, src, c0)
         for j in range(J):
             v_mult(0, j, 0, 0)

@@ -26,10 +26,10 @@ def tile_multiheadlatentattention_pa_v_kernel(
     nc = tc.nc
     with ExitStack() as ctx:
         keep = ctx.enter_context(tc.tile_pool(name="keep", bufs=1))
-        raws = ctx.enter_context(tc.tile_pool(name="raws", bufs=7))
-        prods = ctx.enter_context(tc.tile_pool(name="prods", bufs=14))
+        raws = ctx.enter_context(tc.tile_pool(name="raws", bufs=4))
+        prods = ctx.enter_context(tc.tile_pool(name="prods", bufs=6))
         work = ctx.enter_context(tc.tile_pool(name="work", bufs=2))
-        outs = ctx.enter_context(tc.tile_pool(name="outs", bufs=4))
+        outs = ctx.enter_context(tc.tile_pool(name="outs", bufs=6))
         psum = ctx.enter_context(tc.psum_pool(name="psum", bufs=2))
 
         ident = keep.tile([P, P], F32, name="ident")
@@ -38,70 +38,60 @@ def tile_multiheadlatentattention_pa_v_kernel(
         make_identity(nc, ident_b[:])
         ctx.enter_context(tc.manual_schedule())
 
-        def raw(name):
-            return raws.tile([P, 4096], BF16, name=name, tag="raw", align_bytes=64)
-
         def load_table(src, k):
             nc.sync.dma_start(out=cs[:, k * 2048 : k * 2048 + 2048], in_=src.rearrange("(p j) c -> p (j c)", j=J))
 
-        def load_g(b, h0, dst, k):
+        def load_g(b, h0, k):
             src = grad_out[b].rearrange("h (p j) d -> p h (j d)", j=J)
             nc.sync.dma_start(
-                out=dst[:, k * 2048 : k * 2048 + 2048].rearrange("p (h f) -> p h f", h=4), in_=src[:, h0 : h0 + 4, :]
+                out=gg[b][:, k * 2048 : k * 2048 + 2048].rearrange("p (h f) -> p h f", h=4), in_=src[:, h0 : h0 + 4, :]
             )
 
         def load_wu(g):
-            nc.sync.dma_start(
-                out=wu_raw[:, g * 2048 : g * 2048 + 2048],
-                in_=Wq_up.rearrange("(g p j) l -> g p (j l)", g=2, j=J)[g],
-            )
+            rows = Wq_up.rearrange("(g a t i) l -> g i a t l", g=2, t=4, i=4)
+            for i in range(4):
+                nc.sync.dma_start(
+                    out=wu_raw[i:P:4, g * 2048 : g * 2048 + 2048].rearrange("p (t l) -> p t l", t=4), in_=rows[g, i]
+                )
 
-        def load_rows(src, w0, name):
-            t = raw(name)
-            nc.sync.dma_start(
-                out=t[:].rearrange("p (j w) -> p j w", j=J),
-                in_=src.rearrange("(p j) w -> p j w", j=J)[:, :, w0 : w0 + 1024],
-            )
+        def load_rows(src, name):
+            t = raws.tile([P, 8192], BF16, name=name, tag="raw", align_bytes=64)
+            nc.sync.dma_start(out=t[:], in_=src.rearrange("(p j) w -> p (j w)", j=J))
             return t
 
         cs = keep.tile([P, 4096], BF16, name="cs", align_bytes=64)
-        r0 = raw("r0")
-        wu_raw = raw("wu_raw")
-        load_wu(0)
+        wu_raw = keep.tile([P, 4096], BF16, name="wu_raw", align_bytes=64)
+        gg = [raws.tile([P, 8192], BF16, name="gg", tag="raw", align_bytes=64) for b in range(B)]
         load_table(rope_cos, 0)
-        load_g(0, 8, r0, 0)
+        load_g(0, 8, 0)
+        load_wu(0)
+        load_g(0, 12, 1)
         load_wu(1)
-        load_g(0, 12, r0, 1)
         load_table(rope_sin, 1)
-        d0 = raw("d0")
-        load_g(0, 0, d0, 0)
-        load_g(0, 4, d0, 1)
-        wd_raw = [load_rows(Wq_down, 0, "wd_raw0"), load_rows(Wq_down, 1024, "wd_raw1")]
-        r1 = raw("r1")
-        load_g(1, 8, r1, 0)
-        load_g(1, 12, r1, 1)
-        d1 = raw("d1")
-        load_g(1, 0, d1, 0)
-        load_g(1, 4, d1, 1)
-        x_raw = {}
-        for half in range(2):
-            for b in range(B):
-                x_raw[b, half] = load_rows(hidden_states[b], half * 1024, "x_raw%d%d" % (b, half))
+        load_g(0, 0, 2)
+        load_g(0, 4, 3)
+        wd_raw = load_rows(Wq_down, "wd_raw")
+        load_g(1, 8, 0)
+        load_g(1, 12, 1)
+        load_g(1, 0, 2)
+        load_g(1, 4, 3)
+        x_raw = [load_rows(hidden_states[b], "x_raw") for b in range(B)]
 
         nsin = keep.tile([P, 2048], BF16, name="nsin")
-        cosv = cs[:, 0:2048].rearrange("p (j h d t) -> p j t h d", j=J, h=4, t=4)
-        sinv = cs[:, 2048:4096].rearrange("p (j h d t) -> p j t h d", j=J, h=4, t=4)
-        nsinv = nsin[:].rearrange("p (j h d t) -> p j t h d", j=J, h=4, t=4)
-        grot = [t[:].rearrange("p (k h j d t) -> p k j t h d", k=2, h=4, j=J, t=4) for t in (r0, r1)]
-        gdir = [t[:].rearrange("p (k h j d t) -> p k j t h d", k=2, h=4, j=J, t=4) for t in (d0, d1)]
+        tables = [
+            t.rearrange("p (j h a t i) -> p j h a t i", j=J, h=4, t=4, i=4)
+            for t in (cs[:, 0:2048], cs[:, 2048:4096], nsin[:])
+        ]
+        gv = [t[:].rearrange("p (k h j a t i) -> p k j h a t i", k=4, h=4, j=J, t=4, i=4) for t in gg]
+
+        def copy(eng, out, in_):
+            if eng == "s":
+                nc.scalar.copy(out=out, in_=in_)
+            else:
+                nc.vector.tensor_copy(out=out, in_=in_)
 
         def interleave(eng, dst, src):
-            d = dst.rearrange("p (c i t) -> p c t i", i=4, t=4)
-            s = src.rearrange("p t (c i) -> p c t i", i=4)
-            if eng == "s":
-                nc.scalar.copy(out=d, in_=s)
-            else:
-                nc.vector.tensor_copy(out=d, in_=s)
+            copy(eng, dst.rearrange("p (c i t) -> p c t i", i=4, t=4), src.rearrange("p t (c i) -> p c t i", i=4))
 
         def q_tiles(name, width):
             codes = keep.tile([P, width], U32, name=name + "q", align_bytes=64)
@@ -126,24 +116,27 @@ def tile_multiheadlatentattention_pa_v_kernel(
         def negate():
             nc.vector.tensor_scalar(out=nsin[:], in0=cs[:, 2048:4096], scalar1=-1.0, scalar2=None, op0=MULT)
 
-        def mult(b, j, g, k):
-            c = (cosv, sinv)[k] if g == 0 else (nsinv, cosv)[k]
-            t = prods.tile([P, 4, 4, 32], F32, name="pr", tag="pr", bufs=14)
-            nc.vector.tensor_tensor(out=t[:], in0=grot[b][:, k, j], in1=c[:, j], op=MULT)
-            pr[b, j, g, k] = t
+        def mult(b, jp, g, k):
+            c = tables[(0, 1, 2, 0)[2 * g + k]]
+            js = slice(2 * jp, 2 * jp + 2)
+            t = prods.tile([P, 4, 2, 4, 8, 4], F32, name="pr", tag="pr", bufs=6)
+            nc.vector.tensor_tensor(
+                out=t[:].rearrange("p t j h a i -> p j h a t i"), in0=gv[b][:, k, js], in1=c[:, js], op=MULT
+            )
+            pr[b, jp, g, k] = t
 
         def sort(b, g, half, eng):
-            if half == 0:
-                srt[b, g] = prods.tile([P, J, 4, 4, 32], BF16, name="ps", tag="ps", bufs=2)
+            if (b, g) not in srt:
+                srt[b, g] = prods.tile([P, 4, J, 4, 8, 4], BF16, name="ps", tag="ps", bufs=2)
             js = slice(2 * half, 2 * half + 2)
-            drain(eng, srt[b, g][:, js], gdir[b][:, g, js])
+            copy(eng, srt[b, g][:, :, js].rearrange("p t j h a i -> p j h a t i"), gv[b][:, 2 + g, js])
 
         def turn(b, j, g):
             t = psum.tile([P, 4, P], F32, name="tp", tag="tp", bufs=3)
             for i in range(4):
                 nc.tensor.matmul(
                     out=t[:, i, :],
-                    lhsT=srt[b, g][:, j, i].rearrange("p h d -> p (h d)"),
+                    lhsT=srt[b, g][:, i, j].rearrange("p h a k -> p (h a k)"),
                     rhs=ident_b[:],
                     start=(i == 0),
                     stop=False,
@@ -152,7 +145,7 @@ def tile_multiheadlatentattention_pa_v_kernel(
                 for i in range(4):
                     nc.tensor.matmul(
                         out=t[:, i, :],
-                        lhsT=pr[b, j, g, k][:, i].rearrange("p h d -> p (h d)"),
+                        lhsT=pr[b, j // 2, g, k][:, i, j % 2].rearrange("p h a k -> p (h a k)"),
                         rhs=ident[:],
                         is_transpose=True,
                         start=False,
@@ -167,31 +160,30 @@ def tile_multiheadlatentattention_pa_v_kernel(
                 out=bank["warm"][:], lhsT=src[:, c0 : c0 + P], rhs=src[:, c0 : c0 + N], start=True, stop=True
             )
 
-        def turn_out(b, j, g):
-            if j == 0:
-                z[b, g] = work.tile([P, 2048], BF16, name="z", tag="z", bufs=2, align_bytes=64)
-            nc.scalar.copy(
-                out=z[b, g][:, j * 512 : j * 512 + 512].rearrange("p (r t) -> p r t", t=4),
-                in_=bank[b, j, g][:].rearrange("p t r -> p r t"),
+        def turn_out(b, j, g, eng):
+            if (b, j // 2) not in z:
+                z[b, j // 2] = work.tile([P, 2, 2, 512], BF16, name="z", tag="z", bufs=3, align_bytes=64)
+            copy(
+                eng,
+                z[b, j // 2][:, g, j % 2].rearrange("p (r t) -> p r t", t=4),
+                bank[b, j, g][:].rearrange("p t r -> p r t"),
             )
 
-        def quant_z(b, g, half):
-            if half == 0:
-                zq = work.tile([P, N], U32, name="zq", tag="zq", bufs=4, align_bytes=64)
-                zs = work.tile([P, N], U8, name="zs", tag="zs", bufs=4, align_bytes=64)
-                zz[b, g] = (zq, zs)
-            c = slice(half * 256, half * 256 + 256)
+        def quant_z(b, half):
+            zq = work.tile([P, 2, 256], U32, name="zq", tag="zq", bufs=2, align_bytes=64)
+            zs = work.tile([P, 2, 256], U8, name="zs", tag="zs", bufs=2, align_bytes=64)
+            zz[b, half] = (zq, zs)
             nc.vector.quantize_mx(
-                out=zz[b, g][0][:, c].bitcast(E5),
-                scales=zz[b, g][1][:, c],
-                in_=z[b, g][:, half * 1024 : half * 1024 + 1024],
+                out=zq[:].rearrange("p g w -> p (g w)").bitcast(E5),
+                scales=zs[:].rearrange("p g w -> p (g w)"),
+                in_=z[b, half][:].rearrange("p g j w -> p (g j w)"),
             )
 
-        def mx(out, lhs, m, rhs, c, start, stop):
+        def mx(out, lhs, lhs_s, rhs, c, start, stop):
             nc.tensor.matmul_mx(
                 out=out,
-                lhsT=lhs[0][:, m * P : m * P + P].bitcast(E5),
-                lhsT_scale=lhs[1][:, m * P : m * P + P],
+                lhsT=lhs.bitcast(E5),
+                lhsT_scale=lhs_s,
                 rhs=rhs[0][:, c].bitcast(E4),
                 rhs_scale=rhs[1][:, c],
                 start=start,
@@ -200,12 +192,13 @@ def tile_multiheadlatentattention_pa_v_kernel(
 
         def dh(b, j):
             t = psum.tile([P, LAT], F32, name="dh", tag="dh", bufs=2)
+            c = slice((j % 2) * P, (j % 2) * P + P)
             for g in range(2):
-                mx(t[:], zz[b, g], j, wu[g], slice(0, LAT), g == 0, g == 1)
+                mx(t[:], zz[b, j // 2][0][:, g, c], zz[b, j // 2][1][:, g, c], wu[g], slice(0, LAT), g == 0, g == 1)
             bank["dh", b, j] = t
 
         def dh_out(b, j):
-            if j == 0:
+            if b not in dd:
                 dd[b] = work.tile([P, J, LAT], BF16, name="d", tag="d", bufs=2, align_bytes=64)
             nc.scalar.copy(out=dd[b][:, j, :], in_=bank["dh", b, j][:])
 
@@ -219,8 +212,8 @@ def tile_multiheadlatentattention_pa_v_kernel(
             bank["w", b, half] = t
 
         def words_out(b, half):
-            if half == 0:
-                tt[b] = work.tile([P, 2048], BF16, name="tt", tag="tt", bufs=2, align_bytes=64)
+            if b not in tt:
+                tt[b] = work.tile([P, 2048], BF16, name="tt", tag="tt", bufs=1, align_bytes=64)
             nc.scalar.copy(
                 out=tt[b][:, half * 1024 : half * 1024 + 1024].bitcast(F32).rearrange("p (k r u) -> p k r u", k=2, u=2),
                 in_=bank["w", b, half][:].rearrange("p k u r -> p k r u"),
@@ -233,314 +226,262 @@ def tile_multiheadlatentattention_pa_v_kernel(
             quant(lat[b], slice(0, N), tt[b][:], E5)
 
         def il_tile(key, eng):
-            il[key] = work.tile([P, 2048], BF16, name="il", tag="il" + eng, bufs=3, align_bytes=64)
+            n = 3 if eng == "v" else 2
+            il[key] = work.tile([P, 2048], BF16, name="il", tag="il" + eng, bufs=n, align_bytes=64)
             return il[key][:]
 
-        def il_tok(b):
-            interleave("v", il_tile(("tok", b), "v"), dd[b][:])
+        def il_tok(b, eng):
+            interleave(eng, il_tile(("tok", b), eng), dd[b][:])
 
         def quant_tok(b):
             quant(tok[b], slice(0, N), il["tok", b][:], E5)
 
         def il_wu(g, eng):
-            interleave(eng, il_tile(("wu", g), eng), wu_raw[:, g * 2048 : g * 2048 + 2048].rearrange("p (t w) -> p t w", t=4))
+            interleave(
+                eng, il_tile(("wu", g), eng), wu_raw[:, g * 2048 : g * 2048 + 2048].rearrange("p (t w) -> p t w", t=4)
+            )
 
         def quant_wu(g):
             quant(wu[g], slice(0, LAT), il["wu", g][:], E4)
 
         def il_rows(eng, key, src, n):
             v = src[:].rearrange("p (t w) -> p t w", t=4)
-            interleave(eng, il_tile((key, n), eng), v[:, :, (n % 2) * 512 : (n % 2) * 512 + 512])
+            interleave(eng, il_tile((key, n), eng), v[:, :, n * N : n * N + N])
 
         def il_wd(n, eng):
-            il_rows(eng, "wd", wd_raw[n // 2], n)
+            il_rows(eng, "wd", wd_raw, n)
 
         def quant_wd(n):
             quant(wd, slice(n * N, n * N + N), il["wd", n][:], E4)
 
         def il_x(b, n, eng):
-            il_rows(eng, b, x_raw[b, n // 2], n)
+            il_rows(eng, b, x_raw[b], n)
 
         def quant_x(b, n):
             quant(xx[b], slice(n * N, n * N + N), il[b, n][:], E4)
 
-        def drain(eng, dst, src):
-            if eng == "s":
-                nc.scalar.copy(out=dst, in_=src)
-            else:
-                nc.vector.tensor_copy(out=dst, in_=src)
-
         def out0(b, j, n):
             t = psum.tile([P, N], F32, name="ob", tag="ob", bufs=3)
-            mx(t[:], lat[b], j, wd, slice(n * N, n * N + N), True, True)
+            c = slice(j * P, j * P + P)
+            mx(t[:], lat[b][0][:, c], lat[b][1][:, c], wd, slice(n * N, n * N + N), True, True)
             bank["o0", b, j, n] = t
 
         def out0_out(b, j, n, eng):
             if (b, j, n // 2) not in st:
-                st[b, j, n // 2] = outs.tile([P, 1024], F32, name="st", tag="st", bufs=4)
-            drain(eng, st[b, j, n // 2][:, (n % 2) * N : (n % 2) * N + N], bank["o0", b, j, n][:])
+                st[b, j, n // 2] = outs.tile([P, 1024], F32, name="st", tag="st", bufs=6)
+            copy(eng, st[b, j, n // 2][:, (n % 2) * N : (n % 2) * N + N], bank["o0", b, j, n][:])
 
         def out0_store(b, j, n):
             nc.sync.dma_start(
-                out=out_0[b].rearrange("(p j) w -> p j w", j=J)[:, j, (n - 1) * N : (n + 1) * N], in_=st[b, j, n // 2][:]
+                out=out_0[b].rearrange("(p j) w -> p j w", j=J)[:, j, (n - 1) * N : (n + 1) * N],
+                in_=st[b, j, n // 2][:],
             )
 
         def out1(m, n):
-            t = psum.tile([P, N], F32, name="ob", tag="ob", bufs=3)
+            t = psum.tile([P, N], F32, name="oc", tag="tp", bufs=3)
+            c = slice(m * P, m * P + P)
             for b in range(B):
-                mx(t[:], tok[b], m, xx[b], slice(n * N, n * N + N), b == 0, b == 1)
+                mx(t[:], tok[b][0][:, c], tok[b][1][:, c], xx[b], slice(n * N, n * N + N), b == 0, b == 1)
             bank["o1", m, n] = t
 
         def out1_out(m, n, eng):
-            st["o1", m, n] = outs.tile([P, N], F32, name="s1", tag="s1", bufs=6)
-            drain(eng, st["o1", m, n][:], bank["o1", m, n][:])
+            if ("o1", n) not in st:
+                st["o1", n] = raws.tile([P, 4, N], F32, name="s1", tag="raw", align_bytes=64)
+            copy(eng, st["o1", n][:, m, :], bank["o1", m, n][:])
 
         def out1_store(m, n):
-            nc.sync.dma_start(out=out_1[m * P : m * P + P, n * N : n * N + N], in_=st["o1", m, n][:])
+            nc.sync.dma_start(out=out_1[m * P : m * P + P, n * N : n * N + N], in_=st["o1", n][:, m, :])
 
         vec, sca, ten, dma = [], [], [], []
 
         def put(stream, key, needs, fn, *args):
             stream.append((key, needs, fn, args))
 
-        def v_mult(b, j, g, k):
-            needs = [("neg",)] if (g == 1 and k == 0) else []
-            put(vec, ("mult", b, j, g, k), needs, mult, b, j, g, k)
+        def on(eng):
+            return sca if eng == "s" else vec
 
-        def v_sort(b, g, h):
-            put(vec, ("sort", b, g, h), [], sort, b, g, h, "v")
+        def neg():
+            put(vec, ("neg",), [], negate)
 
-        def s_sort(b, g, h):
-            put(sca, ("sort", b, g, h), [], sort, b, g, h, "s")
+        def mul(b, jp, g, k):
+            put(vec, ("mult", b, jp, g, k), [("neg",)] if (g, k) == (1, 0) else [], mult, b, jp, g, k)
 
-        def v_quant_z(b, h):
-            for g in range(2):
-                put(vec, ("qz", b, g, h), [("zo", b, 2 * h + 1, g)], quant_z, b, g, h)
+        def so(eng, b, g, h):
+            put(on(eng), ("sort", b, g, h), [], sort, b, g, h, eng)
 
-        def v_wu(g):
+        def qz(b, h):
+            needs = [("zo", b, j, g) for j in (2 * h, 2 * h + 1) for g in range(2)]
+            put(vec, ("qz", b, h), needs, quant_z, b, h)
+
+        def iwu(eng, g):
+            put(on(eng), ("ilwu", g), [], il_wu, g, eng)
+
+        def qwu(g):
             put(vec, ("qwu", g), [("ilwu", g)], quant_wu, g)
 
-        def v_wd(n):
+        def iwd(eng, n):
+            put(on(eng), ("ilwd", n), [], il_wd, n, eng)
+
+        def qwd(n):
             put(vec, ("qwd", n), [("ilwd", n)], quant_wd, n)
 
-        def v_x(b, n):
-            put(vec, ("ilx", b, n), [], il_x, b, n, "v")
+        def ix(eng, b, n):
+            put(on(eng), ("ilx", b, n), [], il_x, b, n, eng)
 
-        def v_qx(b, n):
+        def qx(b, n):
             put(vec, ("qx", b, n), [("ilx", b, n)], quant_x, b, n)
 
-        def v_qlat(b):
+        def qlat(b):
             put(vec, ("qlat", b), [("wo", b, 1)], quant_lat, b)
 
-        def v_iltok(b):
-            put(vec, ("iltok", b), [("dho", b, 3)], il_tok, b)
+        def itok(eng, b):
+            put(on(eng), ("iltok", b), [("dho", b, 3)], il_tok, b, eng)
 
-        def v_qtok(b):
+        def qtok(b):
             put(vec, ("qtok", b), [("iltok", b)], quant_tok, b)
 
-        def v_o1(m, n):
-            put(vec, ("o1o", m, n), [("o1", m, n)], out1_out, m, n, "v")
-
-        def v_o0(b, j, n):
-            put(vec, ("o0o", b, j, n), [("o0", b, j, n)], out0_out, b, j, n, "v")
-
-        def v_ilwu(g):
-            put(vec, ("ilwu", g), [], il_wu, g, "v")
-
-        def v_ilwd(n):
-            put(vec, ("ilwd", n), [], il_wd, n, "v")
-
-        def s_wu(g):
-            put(sca, ("ilwu", g), [], il_wu, g, "s")
-
-        def s_wd(n):
-            put(sca, ("ilwd", n), [], il_wd, n, "s")
-
-        def s_x(b, n):
-            put(sca, ("ilx", b, n), [], il_x, b, n, "s")
-
-        def s_z(b, j, g):
-            put(sca, ("zo", b, j, g), [("turn", b, j, g)], turn_out, b, j, g)
-
-        def s_dh(b, j):
-            put(sca, ("dho", b, j), [("dh", b, j)], dh_out, b, j)
-
-        def s_words(b, h):
-            put(sca, ("wo", b, h), [("words", b, h)], words_out, b, h)
-
-        def s_o0(b, j, n):
-            put(sca, ("o0o", b, j, n), [("o0", b, j, n)], out0_out, b, j, n, "s")
-
-        def s_o1(m, n):
-            put(sca, ("o1o", m, n), [("o1", m, n)], out1_out, m, n, "s")
-
-        def t_turn(b, j, g):
-            needs = [("mult", b, j, g, 0), ("mult", b, j, g, 1), ("sort", b, g, j // 2)]
-            if b == 0:
-                put(ten, ("warm", j, g, "t"), needs, warm, r0, 0)
+        def zt(b, j, g, eng="s"):
+            needs = [("mult", b, j // 2, g, 0), ("mult", b, j // 2, g, 1), ("sort", b, g, j // 2)]
             put(ten, ("turn", b, j, g), needs, turn, b, j, g)
-
-        def t_dh(b, j):
-            put(ten, ("dh", b, j), [("qz", b, g, j // 2) for g in range(2)] + [("qwu", 0), ("qwu", 1)], dh, b, j)
-
-        def t_words(b, h):
-            put(ten, ("words", b, h), [("dho", b, 2 * h + 1)], turn_words, b, h)
-
-        def t_o0(b, j, n):
-            put(ten, ("o0", b, j, n), [("qlat", b), ("qwd", n)], out0, b, j, n)
-            if n % 2 == 1:
-                put(dma, ("o0s", b, j, n), [("o0o", b, j, n - 1), ("o0o", b, j, n)], out0_store, b, j, n)
-
-        def t_o1(m, n):
-            put(ten, ("o1", m, n), [("qtok", 0), ("qtok", 1), ("qx", 0, n), ("qx", 1, n)], out1, m, n)
-            put(dma, ("o1s", m, n), [("o1o", m, n)], out1_store, m, n)
-
-        def o0(eng, b, j, n):
-            t_o0(b, j, n)
-            (s_o0 if eng == "s" else v_o0)(b, j, n)
-
-        def o1(eng, m, n):
-            t_o1(m, n)
-            (s_o1 if eng == "s" else v_o1)(m, n)
-
-        def zt(b, j, g):
-            t_turn(b, j, g)
-            s_z(b, j, g)
+            put(on(eng), ("zo", b, j, g), [("turn", b, j, g)], turn_out, b, j, g, eng)
 
         def dhs(b, h):
             for j in (2 * h, 2 * h + 1):
-                t_dh(b, j)
-                s_dh(b, j)
+                put(ten, ("dh", b, j), [("qz", b, h), ("qwu", 0), ("qwu", 1)], dh, b, j)
+                put(sca, ("dho", b, j), [("dh", b, j)], dh_out, b, j)
 
         def ws(b, h):
-            t_words(b, h)
-            s_words(b, h)
+            put(ten, ("words", b, h), [("dho", b, 2 * h), ("dho", b, 2 * h + 1)], turn_words, b, h)
+            put(sca, ("wo", b, h), [("words", b, h)], words_out, b, h)
 
-        for n, (src, c0, times) in enumerate(((r0, 2048, 2), (cs, 2048, 1), (d0, 0, 2), (d0, 2048, 2))):
-            for i in range(times):
+        def o0(eng, b, j, n):
+            put(ten, ("o0", b, j, n), [("qlat", b), ("qwd", n)], out0, b, j, n)
+            put(on(eng), ("o0o", b, j, n), [("o0", b, j, n)], out0_out, b, j, n, eng)
+            if n % 2 == 1:
+                put(dma, ("o0s", b, j, n), [("o0o", b, j, n - 1), ("o0o", b, j, n)], out0_store, b, j, n)
+
+        def o1(eng, m, n):
+            put(ten, ("o1", m, n), [("qtok", 0), ("qtok", 1), ("qx", 0, n), ("qx", 1, n)], out1, m, n)
+            put(on(eng), ("o1o", m, n), [("o1", m, n)], out1_out, m, n, eng)
+            put(dma, ("o1s", m, n), [("o1o", m, n)], out1_store, m, n)
+
+        for n, (src, c0) in enumerate(((gg[0], 0), (gg[0], 2048), (cs, 2048), (gg[0], 4096), (gg[0], 6144))):
+            for i in range(2):
                 put(ten, ("warm", n, i), [], warm, src, c0)
-        for j in range(J):
-            v_mult(0, j, 0, 0)
-        v_wu(0)
-        for j in range(J):
-            v_mult(0, j, 1, 1)
-        put(vec, ("neg",), [], negate)
-        for j in range(J):
-            v_mult(0, j, 0, 1)
-            v_mult(0, j, 1, 0)
-            if j == 1:
-                v_wu(1)
-                v_sort(0, 0, 1)
-                v_sort(0, 1, 1)
-        v_ilwd(0)
-        v_mult(1, 0, 0, 0)
-        v_quant_z(0, 0)
-        v_wd(0)
-        v_mult(1, 0, 0, 1)
-        v_ilwd(1)
-        v_mult(1, 0, 1, 0)
-        v_wd(1)
-        v_quant_z(0, 1)
-        v_mult(1, 0, 1, 1)
-        v_mult(1, 1, 0, 0)
-        v_mult(1, 1, 0, 1)
-        s_wu(0)
-        s_wu(1)
-        s_sort(0, 0, 0)
-        s_sort(0, 1, 0)
-        zt(0, 0, 0)
-        zt(0, 0, 1)
-        zt(0, 1, 0)
-        zt(0, 1, 1)
-        s_wd(2)
-        zt(0, 2, 0)
-        zt(0, 2, 1)
+
+        mul(0, 0, 0, 0)
+        mul(0, 1, 0, 0)
+        iwu("v", 0)
+        mul(0, 0, 1, 1)
+        qwu(0)
+        mul(0, 0, 0, 1)
+        mul(0, 1, 0, 1)
+        neg()
+        mul(0, 0, 1, 0)
+        qwu(1)
+        mul(0, 1, 1, 1)
+        mul(0, 1, 1, 0)
+        iwd("v", 0)
+        mul(1, 0, 0, 0)
+        qz(0, 0)
+        mul(1, 0, 0, 1)
+        qz(0, 1)
+        iwu("s", 1)
+        so("s", 0, 0, 0)
+        so("s", 0, 0, 1)
+        so("s", 0, 1, 0)
+        so("s", 0, 1, 1)
+        for g in range(2):
+            for j in range(4):
+                zt(0, j, g)
         dhs(0, 0)
-        zt(0, 3, 0)
-        ws(0, 0)
-        zt(0, 3, 1)
-        s_sort(1, 0, 0)
         dhs(0, 1)
-        s_sort(1, 1, 0)
+        so("s", 1, 0, 0)
+        ws(0, 0)
         ws(0, 1)
-        for j in range(1, J):
-            if j > 1:
-                v_mult(1, j, 0, 0)
-                v_mult(1, j, 0, 1)
-            if j == 2:
-                v_sort(1, 0, 1)
-                v_ilwd(3)
-            v_mult(1, j, 1, 0)
-            v_mult(1, j, 1, 1)
-            if j == 1:
-                v_wd(2)
-                v_qlat(0)
-            if j == 2:
-                v_wd(3)
-                v_sort(1, 1, 1)
-                v_iltok(0)
-            if j == 3:
-                v_quant_z(1, 0)
-                v_qtok(0)
-        zt(1, 0, 0)
+        so("s", 1, 1, 0)
+        iwd("s", 1)
+        so("v", 1, 0, 1)
+        mul(1, 1, 0, 0)
+        mul(1, 1, 0, 1)
+        so("v", 1, 1, 1)
+        iwd("v", 2)
+        mul(1, 0, 1, 0)
+        mul(1, 0, 1, 1)
+        qlat(0)
+        qwd(1)
+        qwd(0)
+        qwd(2)
+        mul(1, 1, 1, 0)
+        mul(1, 1, 1, 1)
+        iwd("v", 3)
+        ix("v", 0, 0)
+        qwd(3)
+        qz(1, 0)
+        for j in range(4):
+            zt(1, j, 0)
         o0("s", 0, 0, 0)
         o0("s", 0, 0, 1)
-        zt(1, 0, 1)
-        for j in range(1, 3):
-            for g in range(2):
-                zt(1, j, g)
-                o0("s", 0, j, 2 * g)
-                o0("s", 0, j, 2 * g + 1)
-        o0("s", 0, 0, 2)
-        o0("s", 0, 0, 3)
-        zt(1, 3, 0)
+        for j in range(2):
+            zt(1, j, 1)
+            o0("s", 0, 1, j)
+        o0("s", 0, 2, 0)
+        o0("s", 0, 2, 1)
+        zt(1, 2, 1)
         o0("s", 0, 3, 0)
         o0("s", 0, 3, 1)
         zt(1, 3, 1)
-        v_x(0, 0)
-        v_x(1, 0)
-        v_quant_z(1, 1)
-        v_qx(0, 0)
+        o0("v", 0, 0, 2)
+        o0("v", 0, 0, 3)
+        o0("s", 0, 1, 2)
+        qz(1, 1)
+        qx(0, 0)
         dhs(1, 0)
-        o0("s", 0, 3, 2)
-        ws(1, 0)
+        itok("v", 0)
+        o0("s", 0, 1, 3)
+        o0("v", 0, 2, 2)
         dhs(1, 1)
-        o0("s", 0, 3, 3)
+        qtok(0)
+        o0("s", 0, 2, 3)
+        ws(1, 0)
+        ix("v", 1, 0)
         ws(1, 1)
-        v_qx(1, 0)
-        v_x(0, 1)
-        v_iltok(1)
-        v_qlat(1)
-        v_x(1, 1)
-        v_qtok(1)
+        o0("s", 0, 3, 2)
+        o0("s", 0, 3, 3)
+        qlat(1)
+        itok("v", 1)
+        qx(1, 0)
+        qtok(1)
         for n in range(4):
             o0("s", 1, 0, n)
-        v_qx(0, 1)
         for n in range(4):
             o0("s", 1, 1, n)
-        v_qx(1, 1)
-        v_x(0, 2)
+        ix("v", 0, 1)
+        ix("v", 1, 1)
+        qx(0, 1)
+        qx(1, 1)
         for m in range(4):
             o1("s", m, 0)
-        v_x(1, 2)
-        v_qx(0, 2)
+        ix("v", 0, 2)
+        ix("v", 1, 2)
+        qx(0, 2)
+        qx(1, 2)
         for n in range(4):
             o0("s", 1, 2, n)
-        v_qx(1, 2)
-        v_x(0, 3)
+        ix("v", 0, 3)
         for m in range(4):
             o1("s", m, 1)
-        v_x(1, 3)
-        v_qx(0, 3)
-        v_qx(1, 3)
-        for n in range(2):
-            o1("s", 2 * n, 2)
-            o0("v", 1, 3, 2 * n)
-            o1("s", 2 * n + 1, 2)
-            o0("v", 1, 3, 2 * n + 1)
+        ix("v", 1, 3)
+        qx(0, 3)
+        o0("s", 1, 3, 0)
+        o0("s", 1, 3, 1)
         for m in range(4):
-            o1("v" if m % 2 else "s", m, 3)
-
+            o1("s", m, 2)
+        qx(1, 3)
+        o0("v", 1, 3, 2)
+        o0("s", 1, 3, 3)
+        for m in range(4):
+            o1("s" if m == 3 else "v", m, 3)
         done = {}
         streams = [vec, sca, ten, dma]
         at = [0, 0, 0, 0]

from contextlib import ExitStack

import concourse.mybir as mybir
from concourse.masks import make_identity

F32 = mybir.dt.float32
BF16 = mybir.dt.bfloat16
U32 = mybir.dt.uint32
U8 = mybir.dt.uint8
E4 = mybir.dt.float8_e4m3fn_x4
E5 = mybir.dt.float8_e5m2_x4
MULT = mybir.AluOpType.mult

P = 128
B, S, H, LAT, HALF = 2, 512, 2048, 512, 1024
J = 4
N = 512

FLOPS = 2 * B * S * HALF * LAT + 4 * B * S * LAT * H
BYTES = 2 * (B * S * H * 2 + LAT * H + HALF * LAT + 2 * S * 512) + 4 * (B * S * H + LAT * H)


def tile_multiheadlatentattention_pa_v_kernel(
    tc, hidden_states, Wq_down, bq_down, Wq_up, bq_up, rope_cos, rope_sin, q_lat, grad_out, out_0, out_1
):
    nc = tc.nc
    with ExitStack() as ctx:
        keep = ctx.enter_context(tc.tile_pool(name="keep", bufs=1))
        raws = ctx.enter_context(tc.tile_pool(name="raws", bufs=4))
        prods = ctx.enter_context(tc.tile_pool(name="prods", bufs=6))
        work = ctx.enter_context(tc.tile_pool(name="work", bufs=2))
        outs = ctx.enter_context(tc.tile_pool(name="outs", bufs=6))
        psum = ctx.enter_context(tc.psum_pool(name="psum", bufs=2))

        ident = keep.tile([P, P], F32, name="ident")
        make_identity(nc, ident[:])
        ident_b = keep.tile([P, P], BF16, name="ident_b")
        make_identity(nc, ident_b[:])
        ctx.enter_context(tc.manual_schedule())

        def load_table(src, k):
            nc.sync.dma_start(out=cs[:, k * 2048 : k * 2048 + 2048], in_=src.rearrange("(p j) c -> p (j c)", j=J))

        def load_g(b, h0, k):
            src = grad_out[b].rearrange("h (p j) d -> p h (j d)", j=J)
            nc.sync.dma_start(
                out=gg[b][:, k * 2048 : k * 2048 + 2048].rearrange("p (h f) -> p h f", h=4), in_=src[:, h0 : h0 + 4, :]
            )

        def load_wu(g):
            rows = Wq_up.rearrange("(g a t i) l -> g i a t l", g=2, t=4, i=4)
            for i in range(4):
                nc.sync.dma_start(
                    out=wu_raw[i:P:4, g * 2048 : g * 2048 + 2048].rearrange("p (t l) -> p t l", t=4), in_=rows[g, i]
                )

        def load_rows(src, name):
            t = raws.tile([P, 8192], BF16, name=name, tag="raw", align_bytes=64)
            nc.sync.dma_start(out=t[:], in_=src.rearrange("(p j) w -> p (j w)", j=J))
            return t

        cs = keep.tile([P, 4096], BF16, name="cs", align_bytes=64)
        wu_raw = keep.tile([P, 4096], BF16, name="wu_raw", align_bytes=64)
        gg = [raws.tile([P, 8192], BF16, name="gg", tag="raw", align_bytes=64) for b in range(B)]
        load_table(rope_cos, 0)
        load_g(0, 8, 0)
        load_wu(0)
        load_g(0, 12, 1)
        load_wu(1)
        load_table(rope_sin, 1)
        load_g(0, 0, 2)
        load_g(0, 4, 3)
        wd_raw = load_rows(Wq_down, "wd_raw")
        load_g(1, 8, 0)
        load_g(1, 12, 1)
        load_g(1, 0, 2)
        load_g(1, 4, 3)
        x_raw = [load_rows(hidden_states[b], "x_raw") for b in range(B)]

        nsin = keep.tile([P, 2048], BF16, name="nsin")
        tables = [
            t.rearrange("p (j h a t i) -> p j h a t i", j=J, h=4, t=4, i=4)
            for t in (cs[:, 0:2048], cs[:, 2048:4096], nsin[:])
        ]
        gv = [t[:].rearrange("p (k h j a t i) -> p k j h a t i", k=4, h=4, j=J, t=4, i=4) for t in gg]

        def copy(eng, out, in_):
            if eng == "s":
                nc.scalar.copy(out=out, in_=in_)
            else:
                nc.vector.tensor_copy(out=out, in_=in_)

        def interleave(eng, dst, src):
            copy(eng, dst.rearrange("p (c i t) -> p c t i", i=4, t=4), src.rearrange("p t (c i) -> p c t i", i=4))

        def q_tiles(name, width):
            codes = keep.tile([P, width], U32, name=name + "q", align_bytes=64)
            scales = keep.tile([P, width], U8, name=name + "s", align_bytes=64)
            return codes, scales

        wu = [q_tiles("wu%d" % g, LAT) for g in range(2)]
        wd = q_tiles("wd", H)
        xx = [q_tiles("x%d" % b, H) for b in range(B)]
        lat = [q_tiles("lat%d" % b, N) for b in range(B)]
        tok = [q_tiles("tok%d" % b, N) for b in range(B)]
        z = {}
        zz = {}
        pr = {}
        srt = {}
        bank = {}
        il = {}
        dd = {}
        tt = {}
        st = {}

        def negate():
            nc.vector.tensor_scalar(out=nsin[:], in0=cs[:, 2048:4096], scalar1=-1.0, scalar2=None, op0=MULT)

        def mult(b, jp, g, k):
            c = tables[(0, 1, 2, 0)[2 * g + k]]
            js = slice(2 * jp, 2 * jp + 2)
            t = prods.tile([P, 4, 2, 4, 8, 4], F32, name="pr", tag="pr", bufs=6)
            nc.vector.tensor_tensor(
                out=t[:].rearrange("p t j h a i -> p j h a t i"), in0=gv[b][:, k, js], in1=c[:, js], op=MULT
            )
            pr[b, jp, g, k] = t

        def sort(b, g, half, eng):
            if (b, g) not in srt:
                srt[b, g] = prods.tile([P, 4, J, 4, 8, 4], BF16, name="ps", tag="ps", bufs=2)
            js = slice(2 * half, 2 * half + 2)
            copy(eng, srt[b, g][:, :, js].rearrange("p t j h a i -> p j h a t i"), gv[b][:, 2 + g, js])

        def turn(b, j, g):
            t = psum.tile([P, 4, P], F32, name="tp", tag="tp", bufs=3)
            for i in range(4):
                nc.tensor.matmul(
                    out=t[:, i, :],
                    lhsT=srt[b, g][:, i, j].rearrange("p h a k -> p (h a k)"),
                    rhs=ident_b[:],
                    start=(i == 0),
                    stop=False,
                )
            for k in range(2):
                for i in range(4):
                    nc.tensor.matmul(
                        out=t[:, i, :],
                        lhsT=pr[b, j // 2, g, k][:, i, j % 2].rearrange("p h a k -> p (h a k)"),
                        rhs=ident[:],
                        is_transpose=True,
                        start=False,
                        stop=(k == 1 and i == 3),
                    )
            bank[b, j, g] = t

        def warm(src, c0):
            if "warm" not in bank:
                bank["warm"] = psum.tile([P, N], F32, name="warm", tag="dh", bufs=2)
            nc.tensor.matmul(
                out=bank["warm"][:], lhsT=src[:, c0 : c0 + P], rhs=src[:, c0 : c0 + N], start=True, stop=True
            )

        def turn_out(b, j, g, eng):
            if (b, j // 2) not in z:
                z[b, j // 2] = work.tile([P, 2, 2, 512], BF16, name="z", tag="z", bufs=3, align_bytes=64)
            copy(
                eng,
                z[b, j // 2][:, g, j % 2].rearrange("p (r t) -> p r t", t=4),
                bank[b, j, g][:].rearrange("p t r -> p r t"),
            )

        def quant_z(b, half):
            zq = work.tile([P, 2, 256], U32, name="zq", tag="zq", bufs=2, align_bytes=64)
            zs = work.tile([P, 2, 256], U8, name="zs", tag="zs", bufs=2, align_bytes=64)
            zz[b, half] = (zq, zs)
            nc.vector.quantize_mx(
                out=zq[:].rearrange("p g w -> p (g w)").bitcast(E5),
                scales=zs[:].rearrange("p g w -> p (g w)"),
                in_=z[b, half][:].rearrange("p g j w -> p (g j w)"),
            )

        def mx(out, lhs, lhs_s, rhs, c, start, stop):
            nc.tensor.matmul_mx(
                out=out,
                lhsT=lhs.bitcast(E5),
                lhsT_scale=lhs_s,
                rhs=rhs[0][:, c].bitcast(E4),
                rhs_scale=rhs[1][:, c],
                start=start,
                stop=stop,
            )

        def dh(b, j):
            t = psum.tile([P, LAT], F32, name="dh", tag="dh", bufs=2)
            c = slice((j % 2) * P, (j % 2) * P + P)
            for g in range(2):
                mx(t[:], zz[b, j // 2][0][:, g, c], zz[b, j // 2][1][:, g, c], wu[g], slice(0, LAT), g == 0, g == 1)
            bank["dh", b, j] = t

        def dh_out(b, j):
            if b not in dd:
                dd[b] = work.tile([P, J, LAT], BF16, name="d", tag="d", bufs=2, align_bytes=64)
            nc.scalar.copy(out=dd[b][:, j, :], in_=bank["dh", b, j][:])

        def turn_words(b, half):
            words = dd[b][:].rearrange("p j l -> p (j l)").bitcast(F32)
            t = psum.tile([P, 2, 2, P], F32, name="tb", tag="tp", bufs=3)
            for k in range(2):
                for u in range(2):
                    w0 = (2 * half + k) * 256 + u
                    nc.tensor.transpose(t[:, k, u, :], words[:, w0 : w0 + 255 : 2], ident[:])
            bank["w", b, half] = t

        def words_out(b, half):
            if b not in tt:
                tt[b] = work.tile([P, 2048], BF16, name="tt", tag="tt", bufs=1, align_bytes=64)
            nc.scalar.copy(
                out=tt[b][:, half * 1024 : half * 1024 + 1024].bitcast(F32).rearrange("p (k r u) -> p k r u", k=2, u=2),
                in_=bank["w", b, half][:].rearrange("p k u r -> p k r u"),
            )

        def quant(dst, c, src, dt):
            nc.vector.quantize_mx(out=dst[0][:, c].bitcast(dt), scales=dst[1][:, c], in_=src)

        def quant_lat(b):
            quant(lat[b], slice(0, N), tt[b][:], E5)

        def il_tile(key, eng):
            n = 3 if eng == "v" else 2
            il[key] = work.tile([P, 2048], BF16, name="il", tag="il" + eng, bufs=n, align_bytes=64)
            return il[key][:]

        def il_tok(b, eng):
            interleave(eng, il_tile(("tok", b), eng), dd[b][:])

        def quant_tok(b):
            quant(tok[b], slice(0, N), il["tok", b][:], E5)

        def il_wu(g, eng):
            interleave(
                eng, il_tile(("wu", g), eng), wu_raw[:, g * 2048 : g * 2048 + 2048].rearrange("p (t w) -> p t w", t=4)
            )

        def quant_wu(g):
            quant(wu[g], slice(0, LAT), il["wu", g][:], E4)

        def il_rows(eng, key, src, n):
            v = src[:].rearrange("p (t w) -> p t w", t=4)
            interleave(eng, il_tile((key, n), eng), v[:, :, n * N : n * N + N])

        def il_wd(n, eng):
            il_rows(eng, "wd", wd_raw, n)

        def quant_wd(n):
            quant(wd, slice(n * N, n * N + N), il["wd", n][:], E4)

        def il_x(b, n, eng):
            il_rows(eng, b, x_raw[b], n)

        def quant_x(b, n):
            quant(xx[b], slice(n * N, n * N + N), il[b, n][:], E4)

        def out0(b, j, n):
            t = psum.tile([P, N], F32, name="ob", tag="ob", bufs=3)
            c = slice(j * P, j * P + P)
            mx(t[:], lat[b][0][:, c], lat[b][1][:, c], wd, slice(n * N, n * N + N), True, True)
            bank["o0", b, j, n] = t

        def out0_out(b, j, n, eng):
            if (b, j, n // 2) not in st:
                st[b, j, n // 2] = outs.tile([P, 1024], F32, name="st", tag="st", bufs=6)
            copy(eng, st[b, j, n // 2][:, (n % 2) * N : (n % 2) * N + N], bank["o0", b, j, n][:])

        def out0_store(b, j, n):
            nc.sync.dma_start(
                out=out_0[b].rearrange("(p j) w -> p j w", j=J)[:, j, (n - 1) * N : (n + 1) * N],
                in_=st[b, j, n // 2][:],
            )

        def out1(m, n):
            t = psum.tile([P, N], F32, name="oc", tag="tp", bufs=3)
            c = slice(m * P, m * P + P)
            for b in range(B):
                mx(t[:], tok[b][0][:, c], tok[b][1][:, c], xx[b], slice(n * N, n * N + N), b == 0, b == 1)
            bank["o1", m, n] = t

        def out1_out(m, n, eng):
            if ("o1", n) not in st:
                st["o1", n] = raws.tile([P, 4, N], F32, name="s1", tag="raw", align_bytes=64)
            copy(eng, st["o1", n][:, m, :], bank["o1", m, n][:])

        def out1_store(m, n):
            nc.sync.dma_start(out=out_1[m * P : m * P + P, n * N : n * N + N], in_=st["o1", n][:, m, :])

        vec, sca, ten, dma = [], [], [], []

        def put(stream, key, needs, fn, *args):
            stream.append((key, needs, fn, args))

        def on(eng):
            return sca if eng == "s" else vec

        def neg():
            put(vec, ("neg",), [], negate)

        def mul(b, jp, g, k):
            put(vec, ("mult", b, jp, g, k), [("neg",)] if (g, k) == (1, 0) else [], mult, b, jp, g, k)

        def so(eng, b, g, h):
            put(on(eng), ("sort", b, g, h), [], sort, b, g, h, eng)

        def qz(b, h):
            needs = [("zo", b, j, g) for j in (2 * h, 2 * h + 1) for g in range(2)]
            put(vec, ("qz", b, h), needs, quant_z, b, h)

        def iwu(eng, g):
            put(on(eng), ("ilwu", g), [], il_wu, g, eng)

        def qwu(g):
            put(vec, ("qwu", g), [("ilwu", g)], quant_wu, g)

        def iwd(eng, n):
            put(on(eng), ("ilwd", n), [], il_wd, n, eng)

        def qwd(n):
            put(vec, ("qwd", n), [("ilwd", n)], quant_wd, n)

        def ix(eng, b, n):
            put(on(eng), ("ilx", b, n), [], il_x, b, n, eng)

        def qx(b, n):
            put(vec, ("qx", b, n), [("ilx", b, n)], quant_x, b, n)

        def qlat(b):
            put(vec, ("qlat", b), [("wo", b, 1)], quant_lat, b)

        def itok(eng, b):
            put(on(eng), ("iltok", b), [("dho", b, 3)], il_tok, b, eng)

        def qtok(b):
            put(vec, ("qtok", b), [("iltok", b)], quant_tok, b)

        def zt(b, j, g, eng="s"):
            needs = [("mult", b, j // 2, g, 0), ("mult", b, j // 2, g, 1), ("sort", b, g, j // 2)]
            put(ten, ("turn", b, j, g), needs, turn, b, j, g)
            put(on(eng), ("zo", b, j, g), [("turn", b, j, g)], turn_out, b, j, g, eng)

        def dhs(b, h):
            for j in (2 * h, 2 * h + 1):
                put(ten, ("dh", b, j), [("qz", b, h), ("qwu", 0), ("qwu", 1)], dh, b, j)
                put(sca, ("dho", b, j), [("dh", b, j)], dh_out, b, j)

        def ws(b, h):
            put(ten, ("words", b, h), [("dho", b, 2 * h), ("dho", b, 2 * h + 1)], turn_words, b, h)
            put(sca, ("wo", b, h), [("words", b, h)], words_out, b, h)

        def o0(eng, b, j, n):
            put(ten, ("o0", b, j, n), [("qlat", b), ("qwd", n)], out0, b, j, n)
            put(on(eng), ("o0o", b, j, n), [("o0", b, j, n)], out0_out, b, j, n, eng)
            if n % 2 == 1:
                put(dma, ("o0s", b, j, n), [("o0o", b, j, n - 1), ("o0o", b, j, n)], out0_store, b, j, n)

        def o1(eng, m, n):
            put(ten, ("o1", m, n), [("qtok", 0), ("qtok", 1), ("qx", 0, n), ("qx", 1, n)], out1, m, n)
            put(on(eng), ("o1o", m, n), [("o1", m, n)], out1_out, m, n, eng)
            put(dma, ("o1s", m, n), [("o1o", m, n)], out1_store, m, n)

        for n, (src, c0) in enumerate(((gg[0], 0), (gg[0], 2048), (cs, 2048), (gg[0], 4096), (gg[0], 6144))):
            for i in range(2):
                put(ten, ("warm", n, i), [], warm, src, c0)

        mul(0, 0, 0, 0)
        mul(0, 1, 0, 0)
        iwu("v", 0)
        mul(0, 0, 1, 1)
        qwu(0)
        mul(0, 0, 0, 1)
        mul(0, 1, 0, 1)
        neg()
        mul(0, 0, 1, 0)
        qwu(1)
        mul(0, 1, 1, 1)
        mul(0, 1, 1, 0)
        iwd("v", 0)
        mul(1, 0, 0, 0)
        qz(0, 0)
        mul(1, 0, 0, 1)
        qz(0, 1)
        iwu("s", 1)
        so("s", 0, 0, 0)
        so("s", 0, 0, 1)
        so("s", 0, 1, 0)
        so("s", 0, 1, 1)
        for g in range(2):
            for j in range(4):
                zt(0, j, g)
        dhs(0, 0)
        dhs(0, 1)
        so("s", 1, 0, 0)
        ws(0, 0)
        ws(0, 1)
        so("s", 1, 1, 0)
        iwd("s", 1)
        so("v", 1, 0, 1)
        mul(1, 1, 0, 0)
        mul(1, 1, 0, 1)
        so("v", 1, 1, 1)
        iwd("v", 2)
        mul(1, 0, 1, 0)
        mul(1, 0, 1, 1)
        qlat(0)
        qwd(1)
        qwd(0)
        qwd(2)
        mul(1, 1, 1, 0)
        mul(1, 1, 1, 1)
        iwd("v", 3)
        ix("v", 0, 0)
        qwd(3)
        qz(1, 0)
        for j in range(4):
            zt(1, j, 0)
        o0("s", 0, 0, 0)
        o0("s", 0, 0, 1)
        for j in range(2):
            zt(1, j, 1)
            o0("s", 0, 1, j)
        o0("s", 0, 2, 0)
        o0("s", 0, 2, 1)
        zt(1, 2, 1)
        o0("s", 0, 3, 0)
        o0("s", 0, 3, 1)
        zt(1, 3, 1)
        o0("v", 0, 0, 2)
        o0("v", 0, 0, 3)
        o0("s", 0, 1, 2)
        qz(1, 1)
        qx(0, 0)
        dhs(1, 0)
        itok("v", 0)
        o0("s", 0, 1, 3)
        o0("v", 0, 2, 2)
        dhs(1, 1)
        qtok(0)
        o0("s", 0, 2, 3)
        ws(1, 0)
        ix("v", 1, 0)
        ws(1, 1)
        o0("s", 0, 3, 2)
        o0("s", 0, 3, 3)
        qlat(1)
        itok("v", 1)
        qx(1, 0)
        qtok(1)
        for n in range(4):
            o0("s", 1, 0, n)
        for n in range(4):
            o0("s", 1, 1, n)
        ix("v", 0, 1)
        ix("v", 1, 1)
        qx(0, 1)
        qx(1, 1)
        for m in range(4):
            o1("s", m, 0)
        ix("v", 0, 2)
        ix("v", 1, 2)
        qx(0, 2)
        qx(1, 2)
        for n in range(4):
            o0("s", 1, 2, n)
        ix("v", 0, 3)
        for m in range(4):
            o1("s", m, 1)
        ix("v", 1, 3)
        qx(0, 3)
        o0("s", 1, 3, 0)
        o0("s", 1, 3, 1)
        for m in range(4):
            o1("s", m, 2)
        qx(1, 3)
        o0("v", 1, 3, 2)
        o0("s", 1, 3, 3)
        for m in range(4):
            o1("s" if m == 3 else "v", m, 3)
        done = {}
        streams = [vec, sca, ten, dma]
        at = [0, 0, 0, 0]
        while any([at[i] < len(streams[i]) for i in range(4)]):
            before = list(at)
            for i in range(4):
                if at[i] < len(streams[i]):
                    key, needs, fn, args = streams[i][at[i]]
                    if all([k in done for k in needs]):
                        fn(*args)
                        done[key] = True
                        at[i] += 1
            assert at != before, [streams[i][at[i]][:2] for i in range(4) if at[i] < len(streams[i])]
